import numpy as np
import ml_dtypes

BF16 = ml_dtypes.bfloat16


def bf(x):
    return np.asarray(x, np.float32).astype(BF16)


def f32(x):
    return np.asarray(x, np.float32)


def f64(x):
    return np.asarray(x).astype(np.float64)


def striped(idx):
    return np.tile(idx.reshape(-1, 16).T, (8, 1))


H, DH, NS, HD, KD, C, S, N = 4, 128, 128, 512, 1536, 512, 2048, 1024


def setup_inputs():
    q = bf(np.random.standard_normal((HD, NS)))
    kn = bf(np.random.standard_normal((KD, N)))
    w_k = bf(np.random.standard_normal((KD, HD)) / np.sqrt(KD))
    b_k = f32(0.1 * np.random.standard_normal((HD, 1)))
    base = f32(np.random.random((C, S)) * (2.0 / NS))
    return {"q": q, "kn": kn, "w_k": w_k, "b_k": b_k, "base": base, "offs": striped(np.random.permutation(S)[:N])}


def reference(q, kn, w_k, b_k, base, offs):
    idx = offs[:16].T.reshape(-1)
    K = f64(w_k).T @ f64(kn) + f64(b_k)
    sc = np.einsum('hdn,hdj->hnj', f64(q).reshape(H, DH, NS), K.reshape(H, DH, N)) / np.sqrt(DH)
    ex = np.exp(sc)
    r = 1.0 / ex.sum(axis=1, keepdims=True)
    out = f64(base).copy()
    out[:, idx] = (ex * r).reshape(C, N)
    return out

@@ -1,0 +1,87 @@
+import math
+
+import concourse.mybir as mybir
+
+BF16, F32, U16 = mybir.dt.bfloat16, mybir.dt.float32, mybir.dt.uint16
+ACT = mybir.ActivationFunctionType
+MULT = mybir.AluOpType.mult
+
+P = 128
+HEADS = 4
+FEATURES = 1536
+F_BLOCKS = FEATURES // P
+SLOTS = 2048
+ENTRIES = 1024
+PIECE = 512
+PIECES = ENTRIES // PIECE
+PIECE_OFFSET_COLUMNS = PIECE // 16
+
+FLOPS = 2 * FEATURES * HEADS * P * ENTRIES + 2 * HEADS * P * P * ENTRIES
+
+
+def tile_fuser_kernel(tc, q, kn, w_k, b_k, base, offs, out):
+    nc = tc.nc
+    with (
+        tc.tile_pool(name="held", bufs=1) as held,
+        tc.tile_pool(name="work", bufs=2) as work,
+        tc.psum_pool(name="psum", bufs=2) as psum,
+    ):
+        offsets = held.tile([P, ENTRIES // 16], U16, name="offsets")
+        nc.sync.dma_start(offsets[:], offs)
+
+        q_sb = held.tile([P, HEADS, P], BF16, name="q_sb")
+        nc.scalar.dma_start(q_sb[:], q.rearrange("(h d) n -> d h n", d=P))
+        bias_sb = held.tile([P, HEADS], F32, name="bias_sb")
+        with nc.allow_non_contiguous_dma(reason="512 biases, one to a partition and head"):
+            nc.scalar.dma_start(bias_sb[:], b_k.rearrange("(h d) o -> d (h o)", d=P))
+
+        w_sb = [held.tile([P, HEADS * P], BF16, name=f"w_sb{f}") for f in range(F_BLOCKS)]
+        kn_sb = [
+            [held.tile([P, PIECE], BF16, name=f"kn_sb{piece}_{f}") for f in range(F_BLOCKS)]
+            for piece in range(PIECES)
+        ]
+        windows = [held.tile([P, SLOTS], F32, name=f"window{h}") for h in range(HEADS)]
+        for f in range(F_BLOCKS):
+            nc.sync.dma_start(w_sb[f][:], w_k[f * P : (f + 1) * P, :])
+            nc.scalar.dma_start(kn_sb[0][f][:], kn[f * P : (f + 1) * P, 0:PIECE])
+        for h in range(HEADS):
+            nc.sync.dma_start(windows[h][:], base[h * P : (h + 1) * P, :])
+        for f in range(F_BLOCKS):
+            nc.scalar.dma_start(kn_sb[1][f][:], kn[f * P : (f + 1) * P, PIECE : 2 * PIECE])
+
+        ones = held.tile([P, P], BF16, name="ones")
+        nc.vector.memset(ones[:], 1.0)
+
+        for piece in range(PIECES):
+            for h in range(HEADS):
+                k_ps = psum.tile([P, PIECE], F32, name="k_ps")
+                for f in range(F_BLOCKS):
+                    nc.tensor.matmul(
+                        k_ps[:],
+                        w_sb[f][:, h * P : (h + 1) * P],
+                        kn_sb[piece][f][:],
+                        start=(f == 0),
+                        stop=(f == F_BLOCKS - 1),
+                    )
+                k_bf = work.tile([P, PIECE], BF16, name="k_bf")
+                nc.scalar.activation(k_bf[:], k_ps[:], ACT.Identity, bias=bias_sb[:, h : h + 1])
+
+                sc_ps = psum.tile([P, PIECE], F32, name="sc_ps")
+                nc.tensor.matmul(sc_ps[:], q_sb[:, h, :], k_bf[:], start=True, stop=True)
+                ex = work.tile([P, PIECE], F32, name="ex")
+                nc.scalar.activation(ex[:], sc_ps[:], ACT.Exp, scale=1.0 / math.sqrt(P))
+
+                ex_bf = work.tile([P, PIECE], BF16, name="ex_bf")
+                nc.scalar.copy(ex_bf[:], ex[:])
+                sum_ps = psum.tile([P, PIECE], F32, name="sum_ps")
+                nc.tensor.matmul(sum_ps[:], ones[:], ex_bf[:], start=True, stop=True)
+                r = work.tile([P, PIECE], F32, name="r")
+                nc.vector.reciprocal(r[:], sum_ps[:])
+
+                piece_offsets = offsets[
+                    :, piece * PIECE_OFFSET_COLUMNS : (piece + 1) * PIECE_OFFSET_COLUMNS
+                ]
+                nc.vector.tensor_tensor(windows[h][:].indirect(piece_offsets), ex[:], r[:], MULT)
+
+                if piece == PIECES - 1:
+                    nc.sync.dma_start(out[h * P : (h + 1) * P, :], windows[h][:])

@@ -1,10 +1,11 @@
 import math
 
 import concourse.mybir as mybir
+from concourse.masks import make_identity
 
 BF16, F32, U16 = mybir.dt.bfloat16, mybir.dt.float32, mybir.dt.uint16
 ACT = mybir.ActivationFunctionType
-MULT = mybir.AluOpType.mult
+ALU = mybir.AluOpType
 
 P = 128
 HEADS = 4
@@ -14,7 +15,11 @@ SLOTS = 2048
 ENTRIES = 1024
 PIECE = 512
 PIECES = ENTRIES // PIECE
+UNITS = PIECES * HEADS
 PIECE_OFFSET_COLUMNS = PIECE // 16
+J_BLOCKS = PIECE // P
+EARLY_BLOCKS = 2
+LATE_BLOCKS = 6
 
 FLOPS = 2 * FEATURES * HEADS * P * ENTRIES + 2 * HEADS * P * P * ENTRIES
 
@@ -23,65 +28,159 @@ def tile_fuser_kernel(tc, q, kn, w_k, b_k, base, offs, out):
     nc = tc.nc
     with (
         tc.tile_pool(name="held", bufs=1) as held,
-        tc.tile_pool(name="work", bufs=2) as work,
+        tc.tile_pool(name="work", bufs=3) as work,
+        tc.psum_pool(name="k_psum", bufs=3) as k_psum,
+        tc.psum_pool(name="sum_psum", bufs=1) as sum_psum,
         tc.psum_pool(name="psum", bufs=2) as psum,
     ):
-        offsets = held.tile([P, ENTRIES // 16], U16, name="offsets")
-        nc.sync.dma_start(offsets[:], offs)
+        w_blocks = w_k.rearrange("(p c) m -> p c m", c=F_BLOCKS)
+        kn_blocks = kn.rearrange("(p c) j -> p c j", c=F_BLOCKS)
 
-        q_sb = held.tile([P, HEADS, P], BF16, name="q_sb")
-        nc.scalar.dma_start(q_sb[:], q.rearrange("(h d) n -> d h n", d=P))
+        w_sb = []
+        kn_sb = [[] for piece in range(PIECES)]
+
+        for c0 in range(0, F_BLOCKS, EARLY_BLOCKS):
+            w_tile = held.tile([P, EARLY_BLOCKS, HEADS * P], BF16, name=f"w_tile{c0}")
+            nc.sync.dma_start(w_tile[:], w_blocks[:, c0 : c0 + EARLY_BLOCKS, :])
+            kn_tile = held.tile([P, EARLY_BLOCKS, PIECE], BF16, name=f"kn_tile0_{c0}")
+            nc.scalar.dma_start(kn_tile[:], kn_blocks[:, c0 : c0 + EARLY_BLOCKS, 0:PIECE])
+            for c in range(EARLY_BLOCKS):
+                w_sb.append(w_tile[:, c, :])
+                kn_sb[0].append(kn_tile[:, c, :])
+
         bias_sb = held.tile([P, HEADS], F32, name="bias_sb")
         with nc.allow_non_contiguous_dma(reason="512 biases, one to a partition and head"):
-            nc.scalar.dma_start(bias_sb[:], b_k.rearrange("(h d) o -> d (h o)", d=P))
-
-        w_sb = [held.tile([P, HEADS * P], BF16, name=f"w_sb{f}") for f in range(F_BLOCKS)]
-        kn_sb = [
-            [held.tile([P, PIECE], BF16, name=f"kn_sb{piece}_{f}") for f in range(F_BLOCKS)]
-            for piece in range(PIECES)
-        ]
+            nc.sync.dma_start(bias_sb[:], b_k.rearrange("(h d) o -> d (h o)", d=P))
+        q_sb = held.tile([P, HEADS, P], BF16, name="q_sb")
+        nc.sync.dma_start(q_sb[:], q.rearrange("(h d) n -> d h n", d=P))
+        offsets = held.tile([P, ENTRIES // 16], U16, name="offsets")
+        nc.sync.dma_start(offsets[:], offs)
         windows = [held.tile([P, SLOTS], F32, name=f"window{h}") for h in range(HEADS)]
-        for f in range(F_BLOCKS):
-            nc.sync.dma_start(w_sb[f][:], w_k[f * P : (f + 1) * P, :])
-            nc.scalar.dma_start(kn_sb[0][f][:], kn[f * P : (f + 1) * P, 0:PIECE])
         for h in range(HEADS):
             nc.sync.dma_start(windows[h][:], base[h * P : (h + 1) * P, :])
-        for f in range(F_BLOCKS):
-            nc.scalar.dma_start(kn_sb[1][f][:], kn[f * P : (f + 1) * P, PIECE : 2 * PIECE])
+        for c0 in range(0, F_BLOCKS, LATE_BLOCKS):
+            kn_tile = held.tile([P, LATE_BLOCKS, PIECE], BF16, name=f"kn_tile1_{c0}")
+            nc.scalar.dma_start(kn_tile[:], kn_blocks[:, c0 : c0 + LATE_BLOCKS, PIECE : 2 * PIECE])
+            for c in range(LATE_BLOCKS):
+                kn_sb[1].append(kn_tile[:, c, :])
 
-        ones = held.tile([P, P], BF16, name="ones")
-        nc.vector.memset(ones[:], 1.0)
+        identity = held.tile([P, P], F32, name="identity")
+        make_identity(nc, identity[:])
+        ones_f32 = held.tile([P, 1], F32, name="ones_f32")
+        nc.vector.memset(ones_f32[:], 1.0)
+        ones_column = held.tile([P, 1], BF16, name="ones_column")
+        nc.scalar.copy(ones_column[:], ones_f32[:])
+        minus_one = held.tile([P, J_BLOCKS], F32, name="minus_one")
+        nc.gpsimd.memset(minus_one[:], -1.0)
 
-        for piece in range(PIECES):
-            for h in range(HEADS):
-                k_ps = psum.tile([P, PIECE], F32, name="k_ps")
-                for f in range(F_BLOCKS):
-                    nc.tensor.matmul(
-                        k_ps[:],
-                        w_sb[f][:, h * P : (h + 1) * P],
-                        kn_sb[piece][f][:],
-                        start=(f == 0),
-                        stop=(f == F_BLOCKS - 1),
-                    )
-                k_bf = work.tile([P, PIECE], BF16, name="k_bf")
-                nc.scalar.activation(k_bf[:], k_ps[:], ACT.Identity, bias=bias_sb[:, h : h + 1])
+        tiles = [{} for u in range(UNITS)]
+        inv_sqrt_d = 1.0 / math.sqrt(P)
 
-                sc_ps = psum.tile([P, PIECE], F32, name="sc_ps")
-                nc.tensor.matmul(sc_ps[:], q_sb[:, h, :], k_bf[:], start=True, stop=True)
-                ex = work.tile([P, PIECE], F32, name="ex")
-                nc.scalar.activation(ex[:], sc_ps[:], ACT.Exp, scale=1.0 / math.sqrt(P))
+        def project(u, blocks):
+            piece, h = divmod(u, HEADS)
+            if blocks[0] == 0:
+                tiles[u]["k_ps"] = k_psum.tile([P, PIECE], F32, name="k_ps")
+            for c in blocks:
+                nc.tensor.matmul(
+                    tiles[u]["k_ps"][:],
+                    w_sb[c][:, h * P : (h + 1) * P],
+                    kn_sb[piece][c],
+                    start=(c == 0),
+                    stop=(c == F_BLOCKS - 1),
+                )
 
-                ex_bf = work.tile([P, PIECE], BF16, name="ex_bf")
-                nc.scalar.copy(ex_bf[:], ex[:])
-                sum_ps = psum.tile([P, PIECE], F32, name="sum_ps")
-                nc.tensor.matmul(sum_ps[:], ones[:], ex_bf[:], start=True, stop=True)
-                r = work.tile([P, PIECE], F32, name="r")
-                nc.vector.reciprocal(r[:], sum_ps[:])
+        def round_k(u):
+            h = u % HEADS
+            tiles[u]["k_bf"] = work.tile([P, PIECE], BF16, name="k_bf")
+            nc.scalar.activation(
+                tiles[u]["k_bf"][:], tiles[u]["k_ps"][:], ACT.Identity, bias=bias_sb[:, h : h + 1]
+            )
 
-                piece_offsets = offsets[
-                    :, piece * PIECE_OFFSET_COLUMNS : (piece + 1) * PIECE_OFFSET_COLUMNS
-                ]
-                nc.vector.tensor_tensor(windows[h][:].indirect(piece_offsets), ex[:], r[:], MULT)
+        def scores(u):
+            h = u % HEADS
+            tiles[u]["sc_ps"] = psum.tile([P, PIECE], F32, name="sc_ps")
+            nc.tensor.matmul(
+                tiles[u]["sc_ps"][:], q_sb[:, h, :], tiles[u]["k_bf"][:], start=True, stop=True
+            )
 
-                if piece == PIECES - 1:
-                    nc.sync.dma_start(out[h * P : (h + 1) * P, :], windows[h][:])
+        def exp_for_sum(u):
+            tiles[u]["ex_bf"] = work.tile([P, PIECE], BF16, name="ex_bf")
+            nc.scalar.activation(tiles[u]["ex_bf"][:], tiles[u]["sc_ps"][:], ACT.Exp, scale=inv_sqrt_d)
+
+        def sums(u):
+            tiles[u]["sum_ps"] = sum_psum.tile([P, J_BLOCKS], F32, name="sum_ps")
+            for b in range(J_BLOCKS):
+                nc.tensor.matmul(
+                    tiles[u]["sum_ps"][:, b : b + 1],
+                    tiles[u]["ex_bf"][:, b * P : (b + 1) * P],
+                    ones_column[:],
+                    start=True,
+                    stop=True,
+                )
+
+        def reciprocal(u):
+            tiles[u]["sum_column"] = work.tile([P, J_BLOCKS], F32, name="sum_column")
+            nc.scalar.copy(tiles[u]["sum_column"][:], tiles[u]["sum_ps"][:])
+            tiles[u]["r_column"] = work.tile([P, J_BLOCKS], F32, name="r_column")
+            nc.gpsimd.tensor_tensor(
+                tiles[u]["r_column"][:], tiles[u]["sum_column"][:], minus_one[:], ALU.pow
+            )
+
+        def spread_r(u):
+            tiles[u]["r_ps"] = psum.tile([P, PIECE], F32, name="r_ps")
+            for b in range(J_BLOCKS):
+                nc.tensor.transpose(
+                    tiles[u]["r_ps"][:, b * P : (b + 1) * P],
+                    tiles[u]["r_column"][:, b : b + 1].to_broadcast([P, P]),
+                    identity[:],
+                )
+
+        def exp_f32(u):
+            tiles[u]["ex"] = work.tile([P, PIECE], F32, name="ex")
+            nc.scalar.activation(tiles[u]["ex"][:], tiles[u]["sc_ps"][:], ACT.Exp, scale=inv_sqrt_d)
+
+        def copy_r(u):
+            tiles[u]["r"] = work.tile([P, PIECE], F32, name="r")
+            nc.scalar.copy(tiles[u]["r"][:], tiles[u]["r_ps"][:])
+
+        def place(u):
+            piece, h = divmod(u, HEADS)
+            piece_offsets = offsets[
+                :, piece * PIECE_OFFSET_COLUMNS : (piece + 1) * PIECE_OFFSET_COLUMNS
+            ]
+            nc.vector.tensor_tensor(
+                windows[h][:].indirect(piece_offsets), tiles[u]["ex"][:], tiles[u]["r"][:], ALU.mult
+            )
+            if piece == PIECES - 1:
+                nc.sync.dma_start(out[h * P : (h + 1) * P, :], windows[h][:])
+
+
+        for c0 in range(0, F_BLOCKS, EARLY_BLOCKS):
+            for u in (0, 1):
+                project(u, range(c0, c0 + EARLY_BLOCKS))
+
+        third = F_BLOCKS // 3
+        for front in range(UNITS + 1):
+            ahead, back = front + 2, front - 1
+            if front < UNITS:
+                round_k(front)
+            if ahead < UNITS:
+                project(ahead, range(0, third))
+            if back >= 0:
+                spread_r(back)
+                exp_f32(back)
+            if front < UNITS:
+                scores(front)
+            if ahead < UNITS:
+                project(ahead, range(third, 2 * third))
+            if front < UNITS:
+                exp_for_sum(front)
+            if back >= 0:
+                copy_r(back)
+                place(back)
+            if front < UNITS:
+                sums(front)
+            if ahead < UNITS:
+                project(ahead, range(2 * third, F_BLOCKS))
+            if front < UNITS:
+                reciprocal(front)

@@ -20,6 +20,7 @@ PIECE_OFFSET_COLUMNS = PIECE // 16
 J_BLOCKS = PIECE // P
 EARLY_BLOCKS = 2
 LATE_BLOCKS = 6
+BLOCKS_BEFORE_SUMS = 4
 
 FLOPS = 2 * FEATURES * HEADS * P * ENTRIES + 2 * HEADS * P * P * ENTRIES
 
@@ -158,29 +159,26 @@ def tile_fuser_kernel(tc, q, kn, w_k, b_k, base, offs, out):
         for c0 in range(0, F_BLOCKS, EARLY_BLOCKS):
             for u in (0, 1):
                 project(u, range(c0, c0 + EARLY_BLOCKS))
+        round_k(0)
 
-        third = F_BLOCKS // 3
         for front in range(UNITS + 1):
-            ahead, back = front + 2, front - 1
-            if front < UNITS:
-                round_k(front)
-            if ahead < UNITS:
-                project(ahead, range(0, third))
-            if back >= 0:
-                spread_r(back)
-                exp_f32(back)
             if front < UNITS:
                 scores(front)
-            if ahead < UNITS:
-                project(ahead, range(third, 2 * third))
+            if front >= 1:
+                spread_r(front - 1)
+            if front + 2 < UNITS:
+                project(front + 2, range(0, BLOCKS_BEFORE_SUMS))
             if front < UNITS:
                 exp_for_sum(front)
-            if back >= 0:
-                copy_r(back)
-                place(back)
+            if front >= 1:
+                copy_r(front - 1)
+                place(front - 1)
             if front < UNITS:
                 sums(front)
-            if ahead < UNITS:
-                project(ahead, range(2 * third, F_BLOCKS))
+            if front + 2 < UNITS:
+                project(front + 2, range(BLOCKS_BEFORE_SUMS, F_BLOCKS))
             if front < UNITS:
                 reciprocal(front)
+                exp_f32(front)
+            if front + 1 < UNITS:
+                round_k(front + 1)

@@ -20,7 +20,7 @@ PIECE_OFFSET_COLUMNS = PIECE // 16
 J_BLOCKS = PIECE // P
 EARLY_BLOCKS = 2
 LATE_BLOCKS = 6
-BLOCKS_BEFORE_SUMS = 4
+BLOCKS_BEFORE_SUMS = 5
 
 FLOPS = 2 * FEATURES * HEADS * P * ENTRIES + 2 * HEADS * P * P * ENTRIES
 
@@ -71,8 +71,6 @@ def tile_fuser_kernel(tc, q, kn, w_k, b_k, base, offs, out):
         nc.vector.memset(ones_f32[:], 1.0)
         ones_column = held.tile([P, 1], BF16, name="ones_column")
         nc.scalar.copy(ones_column[:], ones_f32[:])
-        minus_one = held.tile([P, J_BLOCKS], F32, name="minus_one")
-        nc.gpsimd.memset(minus_one[:], -1.0)
 
         tiles = [{} for u in range(UNITS)]
         inv_sqrt_d = 1.0 / math.sqrt(P)
@@ -120,12 +118,8 @@ def tile_fuser_kernel(tc, q, kn, w_k, b_k, base, offs, out):
                 )
 
         def reciprocal(u):
-            tiles[u]["sum_column"] = work.tile([P, J_BLOCKS], F32, name="sum_column")
-            nc.scalar.copy(tiles[u]["sum_column"][:], tiles[u]["sum_ps"][:])
             tiles[u]["r_column"] = work.tile([P, J_BLOCKS], F32, name="r_column")
-            nc.gpsimd.tensor_tensor(
-                tiles[u]["r_column"][:], tiles[u]["sum_column"][:], minus_one[:], ALU.pow
-            )
+            nc.vector.reciprocal(tiles[u]["r_column"][:], tiles[u]["sum_ps"][:])
 
         def spread_r(u):
             tiles[u]["r_ps"] = psum.tile([P, PIECE], F32, name="r_ps")
@@ -172,13 +166,14 @@ def tile_fuser_kernel(tc, q, kn, w_k, b_k, base, offs, out):
                 exp_for_sum(front)
             if front >= 1:
                 copy_r(front - 1)
-                place(front - 1)
             if front < UNITS:
                 sums(front)
+                reciprocal(front)
+            if front >= 1:
+                place(front - 1)
             if front + 2 < UNITS:
                 project(front + 2, range(BLOCKS_BEFORE_SUMS, F_BLOCKS))
             if front < UNITS:
-                reciprocal(front)
                 exp_f32(front)
             if front + 1 < UNITS:
                 round_k(front + 1)

@@ -158,18 +158,15 @@ def tile_fuser_kernel(tc, q, kn, w_k, b_k, base, offs, out):
         for front in range(UNITS + 1):
             if front < UNITS:
                 scores(front)
-            if front >= 1:
-                spread_r(front - 1)
             if front + 2 < UNITS:
                 project(front + 2, range(0, BLOCKS_BEFORE_SUMS))
             if front < UNITS:
                 exp_for_sum(front)
-            if front >= 1:
-                copy_r(front - 1)
-            if front < UNITS:
                 sums(front)
                 reciprocal(front)
             if front >= 1:
+                spread_r(front - 1)
+                copy_r(front - 1)
                 place(front - 1)
             if front + 2 < UNITS:
                 project(front + 2, range(BLOCKS_BEFORE_SUMS, F_BLOCKS))

@@ -13,14 +13,13 @@ FEATURES = 1536
 F_BLOCKS = FEATURES // P
 SLOTS = 2048
 ENTRIES = 1024
-PIECE = 512
-PIECES = ENTRIES // PIECE
-UNITS = PIECES * HEADS
-PIECE_OFFSET_COLUMNS = PIECE // 16
-J_BLOCKS = PIECE // P
+HALF = 512
+HALVES = ENTRIES // HALF
+SHORT_RUN = 256
 EARLY_BLOCKS = 2
 LATE_BLOCKS = 6
-BLOCKS_BEFORE_SUMS = 5
+BLOCKS_BEFORE_SCORES = {HALF: 4, SHORT_RUN: 6}
+BLOCKS_BEFORE_SUMS = {HALF: 9, SHORT_RUN: 12}
 
 FLOPS = 2 * FEATURES * HEADS * P * ENTRIES + 2 * HEADS * P * P * ENTRIES
 
@@ -38,13 +37,13 @@ def tile_fuser_kernel(tc, q, kn, w_k, b_k, base, offs, out):
         kn_blocks = kn.rearrange("(p c) j -> p c j", c=F_BLOCKS)
 
         w_sb = []
-        kn_sb = [[] for piece in range(PIECES)]
+        kn_sb = [[] for half in range(HALVES)]
 
         for c0 in range(0, F_BLOCKS, EARLY_BLOCKS):
             w_tile = held.tile([P, EARLY_BLOCKS, HEADS * P], BF16, name=f"w_tile{c0}")
             nc.sync.dma_start(w_tile[:], w_blocks[:, c0 : c0 + EARLY_BLOCKS, :])
-            kn_tile = held.tile([P, EARLY_BLOCKS, PIECE], BF16, name=f"kn_tile0_{c0}")
-            nc.scalar.dma_start(kn_tile[:], kn_blocks[:, c0 : c0 + EARLY_BLOCKS, 0:PIECE])
+            kn_tile = held.tile([P, EARLY_BLOCKS, HALF], BF16, name=f"kn_tile0_{c0}")
+            nc.scalar.dma_start(kn_tile[:], kn_blocks[:, c0 : c0 + EARLY_BLOCKS, 0:HALF])
             for c in range(EARLY_BLOCKS):
                 w_sb.append(w_tile[:, c, :])
                 kn_sb[0].append(kn_tile[:, c, :])
@@ -60,8 +59,8 @@ def tile_fuser_kernel(tc, q, kn, w_k, b_k, base, offs, out):
         for h in range(HEADS):
             nc.sync.dma_start(windows[h][:], base[h * P : (h + 1) * P, :])
         for c0 in range(0, F_BLOCKS, LATE_BLOCKS):
-            kn_tile = held.tile([P, LATE_BLOCKS, PIECE], BF16, name=f"kn_tile1_{c0}")
-            nc.scalar.dma_start(kn_tile[:], kn_blocks[:, c0 : c0 + LATE_BLOCKS, PIECE : 2 * PIECE])
+            kn_tile = held.tile([P, LATE_BLOCKS, HALF], BF16, name=f"kn_tile1_{c0}")
+            nc.scalar.dma_start(kn_tile[:], kn_blocks[:, c0 : c0 + LATE_BLOCKS, HALF : 2 * HALF])
             for c in range(LATE_BLOCKS):
                 kn_sb[1].append(kn_tile[:, c, :])
 
@@ -72,43 +71,48 @@ def tile_fuser_kernel(tc, q, kn, w_k, b_k, base, offs, out):
         ones_column = held.tile([P, 1], BF16, name="ones_column")
         nc.scalar.copy(ones_column[:], ones_f32[:])
 
-        tiles = [{} for u in range(UNITS)]
+        units = [(half, h, 0, HALF) for half in range(HALVES) for h in range(HEADS)]
+        units[-1:] = [(HALVES - 1, HEADS - 1, first, SHORT_RUN) for first in range(0, HALF, SHORT_RUN)]
+        n_units = len(units)
+        tiles = [{} for u in range(n_units)]
         inv_sqrt_d = 1.0 / math.sqrt(P)
 
         def project(u, blocks):
-            piece, h = divmod(u, HEADS)
+            half, h, first, run = units[u]
             if blocks[0] == 0:
-                tiles[u]["k_ps"] = k_psum.tile([P, PIECE], F32, name="k_ps")
+                tiles[u]["k_ps"] = k_psum.tile([P, run], F32, name="k_ps")
             for c in blocks:
                 nc.tensor.matmul(
                     tiles[u]["k_ps"][:],
                     w_sb[c][:, h * P : (h + 1) * P],
-                    kn_sb[piece][c],
+                    kn_sb[half][c][:, first : first + run],
                     start=(c == 0),
                     stop=(c == F_BLOCKS - 1),
                 )
 
         def round_k(u):
-            h = u % HEADS
-            tiles[u]["k_bf"] = work.tile([P, PIECE], BF16, name="k_bf")
+            half, h, first, run = units[u]
+            tiles[u]["k_bf"] = work.tile([P, run], BF16, name="k_bf")
             nc.scalar.activation(
                 tiles[u]["k_bf"][:], tiles[u]["k_ps"][:], ACT.Identity, bias=bias_sb[:, h : h + 1]
             )
 
         def scores(u):
-            h = u % HEADS
-            tiles[u]["sc_ps"] = psum.tile([P, PIECE], F32, name="sc_ps")
+            half, h, first, run = units[u]
+            tiles[u]["sc_ps"] = psum.tile([P, run], F32, name="sc_ps")
             nc.tensor.matmul(
                 tiles[u]["sc_ps"][:], q_sb[:, h, :], tiles[u]["k_bf"][:], start=True, stop=True
             )
 
         def exp_for_sum(u):
-            tiles[u]["ex_bf"] = work.tile([P, PIECE], BF16, name="ex_bf")
+            run = units[u][3]
+            tiles[u]["ex_bf"] = work.tile([P, run], BF16, name="ex_bf")
             nc.scalar.activation(tiles[u]["ex_bf"][:], tiles[u]["sc_ps"][:], ACT.Exp, scale=inv_sqrt_d)
 
         def sums(u):
-            tiles[u]["sum_ps"] = sum_psum.tile([P, J_BLOCKS], F32, name="sum_ps")
-            for b in range(J_BLOCKS):
+            run = units[u][3]
+            tiles[u]["sum_ps"] = sum_psum.tile([P, run // P], F32, name="sum_ps")
+            for b in range(run // P):
                 nc.tensor.matmul(
                     tiles[u]["sum_ps"][:, b : b + 1],
                     tiles[u]["ex_bf"][:, b * P : (b + 1) * P],
@@ -118,12 +122,14 @@ def tile_fuser_kernel(tc, q, kn, w_k, b_k, base, offs, out):
                 )
 
         def reciprocal(u):
-            tiles[u]["r_column"] = work.tile([P, J_BLOCKS], F32, name="r_column")
+            run = units[u][3]
+            tiles[u]["r_column"] = work.tile([P, run // P], F32, name="r_column")
             nc.vector.reciprocal(tiles[u]["r_column"][:], tiles[u]["sum_ps"][:])
 
         def spread_r(u):
-            tiles[u]["r_ps"] = psum.tile([P, PIECE], F32, name="r_ps")
-            for b in range(J_BLOCKS):
+            run = units[u][3]
+            tiles[u]["r_ps"] = psum.tile([P, run], F32, name="r_ps")
+            for b in range(run // P):
                 nc.tensor.transpose(
                     tiles[u]["r_ps"][:, b * P : (b + 1) * P],
                     tiles[u]["r_column"][:, b : b + 1].to_broadcast([P, P]),
@@ -131,46 +137,71 @@ def tile_fuser_kernel(tc, q, kn, w_k, b_k, base, offs, out):
                 )
 
         def exp_f32(u):
-            tiles[u]["ex"] = work.tile([P, PIECE], F32, name="ex")
+            run = units[u][3]
+            tiles[u]["ex"] = work.tile([P, run], F32, name="ex")
             nc.scalar.activation(tiles[u]["ex"][:], tiles[u]["sc_ps"][:], ACT.Exp, scale=inv_sqrt_d)
 
         def copy_r(u):
-            tiles[u]["r"] = work.tile([P, PIECE], F32, name="r")
+            run = units[u][3]
+            tiles[u]["r"] = work.tile([P, run], F32, name="r")
             nc.scalar.copy(tiles[u]["r"][:], tiles[u]["r_ps"][:])
 
         def place(u):
-            piece, h = divmod(u, HEADS)
-            piece_offsets = offsets[
-                :, piece * PIECE_OFFSET_COLUMNS : (piece + 1) * PIECE_OFFSET_COLUMNS
-            ]
+            half, h, first, run = units[u]
+            first_column = (half * HALF + first) // 16
+            run_offsets = offsets[:, first_column : first_column + run // 16]
             nc.vector.tensor_tensor(
-                windows[h][:].indirect(piece_offsets), tiles[u]["ex"][:], tiles[u]["r"][:], ALU.mult
+                windows[h][:].indirect(run_offsets), tiles[u]["ex"][:], tiles[u]["r"][:], ALU.mult
             )
-            if piece == PIECES - 1:
+            if half == HALVES - 1 and first + run == HALF:
                 nc.sync.dma_start(out[h * P : (h + 1) * P, :], windows[h][:])
 
 
         for c0 in range(0, F_BLOCKS, EARLY_BLOCKS):
             for u in (0, 1):
                 project(u, range(c0, c0 + EARLY_BLOCKS))
-        round_k(0)
 
-        for front in range(UNITS + 1):
-            if front < UNITS:
-                scores(front)
-            if front + 2 < UNITS:
-                project(front + 2, range(0, BLOCKS_BEFORE_SUMS))
-            if front < UNITS:
-                exp_for_sum(front)
-                sums(front)
-                reciprocal(front)
-            if front >= 1:
-                spread_r(front - 1)
-                copy_r(front - 1)
-                place(front - 1)
-            if front + 2 < UNITS:
-                project(front + 2, range(BLOCKS_BEFORE_SUMS, F_BLOCKS))
-            if front < UNITS:
-                exp_f32(front)
-            if front + 1 < UNITS:
-                round_k(front + 1)
+        round_k(0)
+        round_k(1)
+        project(2, range(0, 3))
+        scores(0)
+        exp_for_sum(0)
+        project(2, range(3, 5))
+        scores(1)
+        exp_for_sum(1)
+        exp_f32(0)
+        project(2, range(5, 8))
+        sums(0)
+        reciprocal(0)
+        project(2, range(8, 10))
+        sums(1)
+        reciprocal(1)
+        spread_r(0)
+        copy_r(0)
+        place(0)
+        project(2, range(10, F_BLOCKS))
+        exp_f32(1)
+
+        for front in range(2, n_units):
+            following = front + 1 < n_units
+            if following:
+                before_scores = BLOCKS_BEFORE_SCORES[units[front + 1][3]]
+                before_sums = BLOCKS_BEFORE_SUMS[units[front + 1][3]]
+            round_k(front)
+            if following:
+                project(front + 1, range(0, before_scores))
+            scores(front)
+            exp_for_sum(front)
+            exp_f32(front)
+            if following:
+                project(front + 1, range(before_scores, before_sums))
+            sums(front)
+            reciprocal(front)
+            spread_r(front - 1)
+            copy_r(front - 1)
+            place(front - 1)
+            if following and before_sums < F_BLOCKS:
+                project(front + 1, range(before_sums, F_BLOCKS))
+        spread_r(n_units - 1)
+        copy_r(n_units - 1)
+        place(n_units - 1)

@@ -195,10 +195,10 @@ def tile_fuser_kernel(tc, q, kn, w_k, b_k, base, offs, out):
             exp_f32(front)
             if following:
                 project(front + 1, range(before_scores, before_sums))
-            sums(front)
-            reciprocal(front)
             spread_r(front - 1)
             copy_r(front - 1)
+            sums(front)
+            reciprocal(front)
             place(front - 1)
             if following and before_sums < F_BLOCKS:
                 project(front + 1, range(before_sums, F_BLOCKS))

@@ -20,6 +20,7 @@ EARLY_BLOCKS = 2
 LATE_BLOCKS = 6
 BLOCKS_BEFORE_SCORES = {HALF: 4, SHORT_RUN: 6}
 BLOCKS_BEFORE_SUMS = {HALF: 9, SHORT_RUN: 12}
+BLOCKS_FROM_SPREAD_TO_SUMS = {HALF: 1, SHORT_RUN: 0}
 
 FLOPS = 2 * FEATURES * HEADS * P * ENTRIES + 2 * HEADS * P * P * ENTRIES
 
@@ -187,6 +188,7 @@ def tile_fuser_kernel(tc, q, kn, w_k, b_k, base, offs, out):
             if following:
                 before_scores = BLOCKS_BEFORE_SCORES[units[front + 1][3]]
                 before_sums = BLOCKS_BEFORE_SUMS[units[front + 1][3]]
+                before_spread = before_sums - BLOCKS_FROM_SPREAD_TO_SUMS[units[front + 1][3]]
             round_k(front)
             if following:
                 project(front + 1, range(0, before_scores))
@@ -194,9 +196,11 @@ def tile_fuser_kernel(tc, q, kn, w_k, b_k, base, offs, out):
             exp_for_sum(front)
             exp_f32(front)
             if following:
-                project(front + 1, range(before_scores, before_sums))
+                project(front + 1, range(before_scores, before_spread))
             spread_r(front - 1)
             copy_r(front - 1)
+            if following and before_spread < before_sums:
+                project(front + 1, range(before_spread, before_sums))
             sums(front)
             reciprocal(front)
             place(front - 1)

@@ -20,7 +20,7 @@ EARLY_BLOCKS = 2
 LATE_BLOCKS = 6
 BLOCKS_BEFORE_SCORES = {HALF: 4, SHORT_RUN: 6}
 BLOCKS_BEFORE_SUMS = {HALF: 9, SHORT_RUN: 12}
-BLOCKS_FROM_SPREAD_TO_SUMS = {HALF: 1, SHORT_RUN: 0}
+BLOCKS_FROM_SPREAD_TO_SUMS = {HALF: 1, SHORT_RUN: 4}
 
 FLOPS = 2 * FEATURES * HEADS * P * ENTRIES + 2 * HEADS * P * P * ENTRIES
 
@@ -188,17 +188,19 @@ def tile_fuser_kernel(tc, q, kn, w_k, b_k, base, offs, out):
             if following:
                 before_scores = BLOCKS_BEFORE_SCORES[units[front + 1][3]]
                 before_sums = BLOCKS_BEFORE_SUMS[units[front + 1][3]]
-                before_spread = before_sums - BLOCKS_FROM_SPREAD_TO_SUMS[units[front + 1][3]]
+                before_spread = before_sums
+                if units[front][3] == HALF:
+                    before_spread -= BLOCKS_FROM_SPREAD_TO_SUMS[units[front + 1][3]]
             round_k(front)
             if following:
                 project(front + 1, range(0, before_scores))
             scores(front)
             exp_for_sum(front)
-            exp_f32(front)
             if following:
                 project(front + 1, range(before_scores, before_spread))
             spread_r(front - 1)
             copy_r(front - 1)
+            exp_f32(front)
             if following and before_spread < before_sums:
                 project(front + 1, range(before_spread, before_sums))
             sums(front)

@@ -44,7 +44,7 @@ def tile_fuser_kernel(tc, q, kn, w_k, b_k, base, offs, out):
             w_tile = held.tile([P, EARLY_BLOCKS, HEADS * P], BF16, name=f"w_tile{c0}")
             nc.sync.dma_start(w_tile[:], w_blocks[:, c0 : c0 + EARLY_BLOCKS, :])
             kn_tile = held.tile([P, EARLY_BLOCKS, HALF], BF16, name=f"kn_tile0_{c0}")
-            nc.scalar.dma_start(kn_tile[:], kn_blocks[:, c0 : c0 + EARLY_BLOCKS, 0:HALF])
+            nc.sync.dma_start(kn_tile[:], kn_blocks[:, c0 : c0 + EARLY_BLOCKS, 0:HALF])
             for c in range(EARLY_BLOCKS):
                 w_sb.append(w_tile[:, c, :])
                 kn_sb[0].append(kn_tile[:, c, :])
@@ -57,13 +57,15 @@ def tile_fuser_kernel(tc, q, kn, w_k, b_k, base, offs, out):
         offsets = held.tile([P, ENTRIES // 16], U16, name="offsets")
         nc.sync.dma_start(offsets[:], offs)
         windows = [held.tile([P, SLOTS], F32, name=f"window{h}") for h in range(HEADS)]
-        for h in range(HEADS):
+        for h in range(2):
             nc.sync.dma_start(windows[h][:], base[h * P : (h + 1) * P, :])
         for c0 in range(0, F_BLOCKS, LATE_BLOCKS):
             kn_tile = held.tile([P, LATE_BLOCKS, HALF], BF16, name=f"kn_tile1_{c0}")
-            nc.scalar.dma_start(kn_tile[:], kn_blocks[:, c0 : c0 + LATE_BLOCKS, HALF : 2 * HALF])
+            nc.sync.dma_start(kn_tile[:], kn_blocks[:, c0 : c0 + LATE_BLOCKS, HALF : 2 * HALF])
             for c in range(LATE_BLOCKS):
                 kn_sb[1].append(kn_tile[:, c, :])
+        for h in range(2, HEADS):
+            nc.sync.dma_start(windows[h][:], base[h * P : (h + 1) * P, :])
 
         identity = held.tile([P, P], F32, name="identity")
         make_identity(nc, identity[:])

@@ -16,7 +16,7 @@ ENTRIES = 1024
 HALF = 512
 HALVES = ENTRIES // HALF
 SHORT_RUN = 256
-EARLY_BLOCKS = 2
+EARLY_LOADS = ((0, 2), (2, 2), (4, 4), (8, 4))
 LATE_BLOCKS = 6
 BLOCKS_BEFORE_SCORES = {HALF: 4, SHORT_RUN: 6}
 BLOCKS_BEFORE_SUMS = {HALF: 9, SHORT_RUN: 12}
@@ -40,12 +40,12 @@ def tile_fuser_kernel(tc, q, kn, w_k, b_k, base, offs, out):
         w_sb = []
         kn_sb = [[] for half in range(HALVES)]
 
-        for c0 in range(0, F_BLOCKS, EARLY_BLOCKS):
-            w_tile = held.tile([P, EARLY_BLOCKS, HEADS * P], BF16, name=f"w_tile{c0}")
-            nc.sync.dma_start(w_tile[:], w_blocks[:, c0 : c0 + EARLY_BLOCKS, :])
-            kn_tile = held.tile([P, EARLY_BLOCKS, HALF], BF16, name=f"kn_tile0_{c0}")
-            nc.sync.dma_start(kn_tile[:], kn_blocks[:, c0 : c0 + EARLY_BLOCKS, 0:HALF])
-            for c in range(EARLY_BLOCKS):
+        for c0, blocks in EARLY_LOADS:
+            w_tile = held.tile([P, blocks, HEADS * P], BF16, name=f"w_tile{c0}")
+            nc.sync.dma_start(w_tile[:], w_blocks[:, c0 : c0 + blocks, :])
+            kn_tile = held.tile([P, blocks, HALF], BF16, name=f"kn_tile0_{c0}")
+            nc.sync.dma_start(kn_tile[:], kn_blocks[:, c0 : c0 + blocks, 0:HALF])
+            for c in range(blocks):
                 w_sb.append(w_tile[:, c, :])
                 kn_sb[0].append(kn_tile[:, c, :])
 
@@ -160,9 +160,9 @@ def tile_fuser_kernel(tc, q, kn, w_k, b_k, base, offs, out):
                 nc.sync.dma_start(out[h * P : (h + 1) * P, :], windows[h][:])
 
 
-        for c0 in range(0, F_BLOCKS, EARLY_BLOCKS):
+        for c0, blocks in EARLY_LOADS:
             for u in (0, 1):
-                project(u, range(c0, c0 + EARLY_BLOCKS))
+                project(u, range(c0, c0 + blocks))
 
         round_k(0)
         round_k(1)

import math

import concourse.mybir as mybir
from concourse.masks import make_identity

BF16, F32, U16 = mybir.dt.bfloat16, mybir.dt.float32, mybir.dt.uint16
ACT = mybir.ActivationFunctionType
ALU = mybir.AluOpType

P = 128
HEADS = 4
FEATURES = 1536
F_BLOCKS = FEATURES // P
SLOTS = 2048
ENTRIES = 1024
HALF = 512
HALVES = ENTRIES // HALF
SHORT_RUN = 256
EARLY_LOADS = ((0, 2), (2, 2), (4, 4), (8, 4))
LATE_BLOCKS = 6
BLOCKS_BEFORE_SCORES = {HALF: 4, SHORT_RUN: 6}
BLOCKS_BEFORE_SUMS = {HALF: 9, SHORT_RUN: 12}
BLOCKS_FROM_SPREAD_TO_SUMS = {HALF: 1, SHORT_RUN: 4}

FLOPS = 2 * FEATURES * HEADS * P * ENTRIES + 2 * HEADS * P * P * ENTRIES


def tile_fuser_kernel(tc, q, kn, w_k, b_k, base, offs, out):
    nc = tc.nc
    with (
        tc.tile_pool(name="held", bufs=1) as held,
        tc.tile_pool(name="work", bufs=3) as work,
        tc.psum_pool(name="k_psum", bufs=3) as k_psum,
        tc.psum_pool(name="sum_psum", bufs=1) as sum_psum,
        tc.psum_pool(name="psum", bufs=2) as psum,
    ):
        w_blocks = w_k.rearrange("(p c) m -> p c m", c=F_BLOCKS)
        kn_blocks = kn.rearrange("(p c) j -> p c j", c=F_BLOCKS)

        w_sb = []
        kn_sb = [[] for half in range(HALVES)]

        for c0, blocks in EARLY_LOADS:
            w_tile = held.tile([P, blocks, HEADS * P], BF16, name=f"w_tile{c0}")
            nc.sync.dma_start(w_tile[:], w_blocks[:, c0 : c0 + blocks, :])
            kn_tile = held.tile([P, blocks, HALF], BF16, name=f"kn_tile0_{c0}")
            nc.sync.dma_start(kn_tile[:], kn_blocks[:, c0 : c0 + blocks, 0:HALF])
            for c in range(blocks):
                w_sb.append(w_tile[:, c, :])
                kn_sb[0].append(kn_tile[:, c, :])

        bias_sb = held.tile([P, HEADS], F32, name="bias_sb")
        with nc.allow_non_contiguous_dma(reason="512 biases, one to a partition and head"):
            nc.sync.dma_start(bias_sb[:], b_k.rearrange("(h d) o -> d (h o)", d=P))
        q_sb = held.tile([P, HEADS, P], BF16, name="q_sb")
        nc.sync.dma_start(q_sb[:], q.rearrange("(h d) n -> d h n", d=P))
        offsets = held.tile([P, ENTRIES // 16], U16, name="offsets")
        nc.sync.dma_start(offsets[:], offs)
        windows = [held.tile([P, SLOTS], F32, name=f"window{h}") for h in range(HEADS)]
        for h in range(2):
            nc.sync.dma_start(windows[h][:], base[h * P : (h + 1) * P, :])
        for c0 in range(0, F_BLOCKS, LATE_BLOCKS):
            kn_tile = held.tile([P, LATE_BLOCKS, HALF], BF16, name=f"kn_tile1_{c0}")
            nc.sync.dma_start(kn_tile[:], kn_blocks[:, c0 : c0 + LATE_BLOCKS, HALF : 2 * HALF])
            for c in range(LATE_BLOCKS):
                kn_sb[1].append(kn_tile[:, c, :])
        for h in range(2, HEADS):
            nc.sync.dma_start(windows[h][:], base[h * P : (h + 1) * P, :])

        identity = held.tile([P, P], F32, name="identity")
        make_identity(nc, identity[:])
        ones_f32 = held.tile([P, 1], F32, name="ones_f32")
        nc.vector.memset(ones_f32[:], 1.0)
        ones_column = held.tile([P, 1], BF16, name="ones_column")
        nc.scalar.copy(ones_column[:], ones_f32[:])

        units = [(half, h, 0, HALF) for half in range(HALVES) for h in range(HEADS)]
        units[-1:] = [(HALVES - 1, HEADS - 1, first, SHORT_RUN) for first in range(0, HALF, SHORT_RUN)]
        n_units = len(units)
        tiles = [{} for u in range(n_units)]
        inv_sqrt_d = 1.0 / math.sqrt(P)

        def project(u, blocks):
            half, h, first, run = units[u]
            if blocks[0] == 0:
                tiles[u]["k_ps"] = k_psum.tile([P, run], F32, name="k_ps")
            for c in blocks:
                nc.tensor.matmul(
                    tiles[u]["k_ps"][:],
                    w_sb[c][:, h * P : (h + 1) * P],
                    kn_sb[half][c][:, first : first + run],
                    start=(c == 0),
                    stop=(c == F_BLOCKS - 1),
                )

        def round_k(u):
            half, h, first, run = units[u]
            tiles[u]["k_bf"] = work.tile([P, run], BF16, name="k_bf")
            nc.scalar.activation(
                tiles[u]["k_bf"][:], tiles[u]["k_ps"][:], ACT.Identity, bias=bias_sb[:, h : h + 1]
            )

        def scores(u):
            half, h, first, run = units[u]
            tiles[u]["sc_ps"] = psum.tile([P, run], F32, name="sc_ps")
            nc.tensor.matmul(
                tiles[u]["sc_ps"][:], q_sb[:, h, :], tiles[u]["k_bf"][:], start=True, stop=True
            )

        def exp_for_sum(u):
            run = units[u][3]
            tiles[u]["ex_bf"] = work.tile([P, run], BF16, name="ex_bf")
            nc.scalar.activation(tiles[u]["ex_bf"][:], tiles[u]["sc_ps"][:], ACT.Exp, scale=inv_sqrt_d)

        def sums(u):
            run = units[u][3]
            tiles[u]["sum_ps"] = sum_psum.tile([P, run // P], F32, name="sum_ps")
            for b in range(run // P):
                nc.tensor.matmul(
                    tiles[u]["sum_ps"][:, b : b + 1],
                    tiles[u]["ex_bf"][:, b * P : (b + 1) * P],
                    ones_column[:],
                    start=True,
                    stop=True,
                )

        def reciprocal(u):
            run = units[u][3]
            tiles[u]["r_column"] = work.tile([P, run // P], F32, name="r_column")
            nc.vector.reciprocal(tiles[u]["r_column"][:], tiles[u]["sum_ps"][:])

        def spread_r(u):
            run = units[u][3]
            tiles[u]["r_ps"] = psum.tile([P, run], F32, name="r_ps")
            for b in range(run // P):
                nc.tensor.transpose(
                    tiles[u]["r_ps"][:, b * P : (b + 1) * P],
                    tiles[u]["r_column"][:, b : b + 1].to_broadcast([P, P]),
                    identity[:],
                )

        def exp_f32(u):
            run = units[u][3]
            tiles[u]["ex"] = work.tile([P, run], F32, name="ex")
            nc.scalar.activation(tiles[u]["ex"][:], tiles[u]["sc_ps"][:], ACT.Exp, scale=inv_sqrt_d)

        def copy_r(u):
            run = units[u][3]
            tiles[u]["r"] = work.tile([P, run], F32, name="r")
            nc.scalar.copy(tiles[u]["r"][:], tiles[u]["r_ps"][:])

        def place(u):
            half, h, first, run = units[u]
            first_column = (half * HALF + first) // 16
            run_offsets = offsets[:, first_column : first_column + run // 16]
            nc.vector.tensor_tensor(
                windows[h][:].indirect(run_offsets), tiles[u]["ex"][:], tiles[u]["r"][:], ALU.mult
            )
            if half == HALVES - 1 and first + run == HALF:
                nc.sync.dma_start(out[h * P : (h + 1) * P, :], windows[h][:])


        for c0, blocks in EARLY_LOADS:
            for u in (0, 1):
                project(u, range(c0, c0 + blocks))

        round_k(0)
        round_k(1)
        project(2, range(0, 3))
        scores(0)
        exp_for_sum(0)
        project(2, range(3, 5))
        scores(1)
        exp_for_sum(1)
        exp_f32(0)
        project(2, range(5, 8))
        sums(0)
        reciprocal(0)
        project(2, range(8, 10))
        sums(1)
        reciprocal(1)
        spread_r(0)
        copy_r(0)
        place(0)
        project(2, range(10, F_BLOCKS))
        exp_f32(1)

        for front in range(2, n_units):
            following = front + 1 < n_units
            if following:
                before_scores = BLOCKS_BEFORE_SCORES[units[front + 1][3]]
                before_sums = BLOCKS_BEFORE_SUMS[units[front + 1][3]]
                before_spread = before_sums
                if units[front][3] == HALF:
                    before_spread -= BLOCKS_FROM_SPREAD_TO_SUMS[units[front + 1][3]]
            round_k(front)
            if following:
                project(front + 1, range(0, before_scores))
            scores(front)
            exp_for_sum(front)
            if following:
                project(front + 1, range(before_scores, before_spread))
            spread_r(front - 1)
            copy_r(front - 1)
            exp_f32(front)
            if following and before_spread < before_sums:
                project(front + 1, range(before_spread, before_sums))
            sums(front)
            reciprocal(front)
            place(front - 1)
            if following and before_sums < F_BLOCKS:
                project(front + 1, range(before_sums, F_BLOCKS))
        spread_r(n_units - 1)
        copy_r(n_units - 1)
        place(n_units - 1)
